import numpy as np
import ml_dtypes


def mxq(x, axis, fmt="e4m3"):
    dtype, down = {"e4m3": (ml_dtypes.float8_e4m3fn, 7), "e5m2": (ml_dtypes.float8_e5m2, 14)}[fmt]
    v = np.moveaxis(np.asarray(x, np.float32).astype(ml_dtypes.bfloat16).astype(np.float64), axis, -1)
    blocks = v.reshape(v.shape[:-1] + (-1, 32))
    amax = np.abs(blocks).max(-1, keepdims=True)
    byte = np.maximum(np.where(amax > 0, np.frexp(amax)[1] - 1 + 127, 0) - down, 1)
    scale = np.exp2(byte - 127.0)
    codes = (blocks / scale).astype(np.float32).astype(dtype).astype(np.float64)
    return np.moveaxis((codes * scale).reshape(v.shape), -1, axis)


WIDE = False


def mx_kscale(k):
    if not WIDE:
        return np.ones(k)
    levels = np.array([10, -10, 5, -5, 0])
    if k % 512:
        return np.exp2(np.random.permutation(np.resize(levels, k // 32))).repeat(32)
    a = np.empty((k // 512, 16))
    for p in range(k // 512):
        a[p, :8] = np.random.permutation(np.resize(levels, 8))
        for g in range(8):
            far = levels[np.abs(levels - a[p, g]) >= 10]
            a[p, g + 8] = far[np.random.randint(len(far))]
    return np.exp2(a.ravel()).repeat(32)


BF16 = ml_dtypes.bfloat16


def bf(x):
    return np.asarray(x, np.float32).astype(BF16)


def f64(x):
    return np.asarray(x).astype(np.float64)


B, S, IN_DIM, OUT_DIM, MOD_DIM = 4, 512, 512, 512, 512
EPS = 1e-8
GAIN = np.sqrt(2.0 / (1.0 + 0.2 ** 2))


def setup_inputs():
    ks = mx_kscale(MOD_DIM)
    kt = mx_kscale(IN_DIM)
    return {"x": bf(np.random.standard_normal((B, S, IN_DIM))),
            "modulation": bf(np.random.standard_normal((B, S, MOD_DIM)) * ks),
            "weight": bf(np.random.standard_normal((OUT_DIM, IN_DIM)) * GAIN / np.sqrt(IN_DIM) / kt[None, :]),
            "bias": bf(np.random.standard_normal(OUT_DIM) * 0.1),
            "mod_w": bf(np.random.standard_normal((IN_DIM, MOD_DIM)) / np.sqrt(MOD_DIM) * kt[:, None] / ks[None, :]),
            "mod_b": bf((1.0 + 0.1 * np.random.standard_normal(IN_DIM)) * kt)}


def reference(x, modulation, weight, bias, mod_w, mod_b):
    xf, w = f64(x), f64(weight)
    s = (mxq(f64(modulation), 2, "e4m3") @ mxq(f64(mod_w), 1, "e4m3").T) + f64(mod_b)
    out = mxq(xf * s, 2, "e4m3") @ mxq(w, 1, "e4m3").T
    demod = 1.0 / np.sqrt((mxq(s * s, 2, "e4m3") @ mxq(w * w, 1, "e4m3").T) + EPS)
    return out * demod + f64(bias)

@@ -1,0 +1,349 @@
+from contextlib import ExitStack
+
+import concourse.mybir as mybir
+from concourse.masks import make_identity
+
+F32 = mybir.dt.float32
+BF16 = mybir.dt.bfloat16
+U32 = mybir.dt.uint32
+U8 = mybir.dt.uint8
+FP8X4 = mybir.dt.float8_e4m3fn_x4
+ACT = mybir.ActivationFunctionType
+ALU = mybir.AluOpType
+
+P = 128
+DIM = 512
+NT = 16
+NU = 8
+FLOPS = 3 * 2 * 2048 * 512 * 512
+
+WARM_A = 4
+WARM_B = 2
+PIN_START = False
+PIN_LOOP = True
+LATE_V = ((6, 1), (7, 0), (7, 1))
+CMOD_S = (0,)
+
+
+def tile_modulatedlinear_kernel(tc, x, modulation, weight, bias, mod_w, mod_b, out):
+    nc = tc.nc
+    with ExitStack() as ctx:
+        const = ctx.enter_context(tc.tile_pool(name="const", bufs=1))
+        work = ctx.enter_context(tc.tile_pool(name="work", bufs=2))
+        psum = ctx.enter_context(tc.psum_pool(name="psum", bufs=1))
+        if PIN_START:
+            ctx.enter_context(tc.manual_schedule())
+
+        xv = x.flatten_outer_dims().rearrange("(p j) i -> p j i", j=NT)
+        mv = modulation.flatten_outer_dims().rearrange("(p j) i -> p j i", j=NT)
+        ov = out.flatten_outer_dims().rearrange("(p j) o -> p j o", j=NT)
+        mwv = mod_w.rearrange("(p c) m -> p c m", c=4)
+
+        x_sb = const.tile([P, NT, DIM], BF16, name="x_sb")
+        m_sb = const.tile([P, NT, DIM], BF16, name="m_sb")
+        mw_sb = const.tile([P, 4, DIM], BF16, name="mw_sb")
+        w_sb = const.tile([P, 4, DIM], BF16, name="w_sb")
+        mb_raw = const.tile([P, 4], BF16, name="mb_raw")
+        brow = const.tile([P, DIM], BF16, name="brow")
+        ones = const.tile([P, P], BF16, name="ones")
+        ident = const.tile([P, P], F32, name="ident")
+        warm = const.tile([P, 1], F32, name="warm")
+        dz = const.tile([P, DIM], BF16, name="dz")
+
+        nc.vector.memset(ones[:], 1.0)
+        nc.vector.memset(dz[:], 0.0)
+        nc.vector.memset(warm[:], 1.0)
+        make_identity(nc, ident[:])
+        nc.vector.memset(brow[:], 0.0)
+
+        def load_m(lo, hi):
+            nc.sync.dma_start(out=m_sb[:, lo:hi, :], in_=mv[:, lo:hi, :])
+
+        def load_x(lo, hi):
+            nc.sync.dma_start(out=x_sb[:, lo:hi, :], in_=xv[:, lo:hi, :])
+
+        load_m(0, 2)
+        for u in range(2):
+            nc.sync.dma_start(out=mw_sb[:, 2 * u:2 * u + 2, :], in_=mwv[:, 2 * u:2 * u + 2, :])
+        nc.scalar.dma_start(out=mb_raw[:], in_=mod_b.rearrange("(p c) -> p c", c=4))
+        nc.scalar.dma_start(out=brow[0:1, :], in_=bias.rearrange("(a n) -> a n", a=1))
+        nc.scalar.activation(out=warm[:], in_=warm[:], func=ACT.Abs_reciprocal_sqrt, bias=1e-8, scale=1.0)
+        nc.sync.dma_start(out=w_sb[:], in_=weight.rearrange("(c p) i -> p c i", p=P))
+        load_m(2, 4)
+        load_x(0, 2)
+        load_x(2, 4)
+        load_m(4, 8)
+        load_x(4, 8)
+        load_m(8, 16)
+        load_x(8, 16)
+
+        def bank(tag):
+            return psum.tile([P, 512], F32, name=tag, tag=tag)
+
+        modb = const.tile([P, 4], F32, name="modb")
+        mwg = const.tile([P, 2048], BF16, name="mwg", align_bytes=64)
+        mw_codes = const.tile([P, 512], U32, name="mw_codes", align_bytes=64)
+        mw_scales = const.tile([P, 512], U8, name="mw_scales", align_bytes=64)
+        wg = const.tile([P, 2048], BF16, name="wg", align_bytes=64)
+        w2g = const.tile([P, 2048], BF16, name="w2g", align_bytes=64)
+        w_codes = const.tile([P, 512], U32, name="w_codes", align_bytes=64)
+        w_scales = const.tile([P, 512], U8, name="w_scales", align_bytes=64)
+        w2_codes = const.tile([P, 512], U32, name="w2_codes", align_bytes=64)
+        w2_scales = const.tile([P, 512], U8, name="w2_scales", align_bytes=64)
+        bias_bc = const.tile([P, DIM], F32, name="bias_bc")
+
+        T = {}
+
+        def copy_on(vector, dst, src):
+            if vector:
+                nc.vector.tensor_copy(out=dst, in_=src)
+            else:
+                nc.scalar.copy(out=dst, in_=src)
+
+        def mw_transposes(b):
+            t = bank(("y0", "q0")[b])
+            for c2 in range(2):
+                words = mw_sb[:, 2 * b + c2, :].bitcast(F32)
+                for v in range(2):
+                    col = (c2 * 2 + v) * P
+                    nc.tensor.transpose(t[:, col:col + P], words[:, v:2 * P:2], ident[:])
+            T[("mwt", b)] = t
+
+        def mw_copy(b, vector):
+            copy_on(
+                vector,
+                mwg[:].bitcast(F32)[:, b * 512:(b + 1) * 512].rearrange("p (c i v) -> p c i v", c=2, v=2),
+                T[("mwt", b)][:].rearrange("p (c v i) -> p c i v", c=2, v=2),
+            )
+
+        def mw_quant(b):
+            nc.vector.quantize_mx(
+                out=mw_codes[:, b * 256:(b + 1) * 256].bitcast(FP8X4),
+                scales=mw_scales[:, b * 256:(b + 1) * 256],
+                in_=mwg[:, b * 1024:(b + 1) * 1024],
+            )
+
+        def w_transposes():
+            wt = [bank("y1"), bank("q1")]
+            for oc in range(4):
+                words = w_sb[:, oc, :].bitcast(F32)
+                for u in range(2):
+                    col = u * 256 + (oc % 2) * P
+                    nc.tensor.transpose(wt[oc // 2][:, col:col + P], words[:, u:2 * P:2], ident[:])
+            T["wt"] = wt
+
+        def w_copy(b, vector):
+            copy_on(
+                vector,
+                wg[:].bitcast(F32)[:, b * 512:(b + 1) * 512].rearrange("p (o u) -> p o u", u=2),
+                T["wt"][b][:].rearrange("p (u o) -> p o u", u=2),
+            )
+
+        def w_square(b):
+            half = slice(b * 1024, (b + 1) * 1024)
+            nc.vector.tensor_tensor(out=w2g[:, half], in0=wg[:, half], in1=wg[:, half], op=ALU.mult)
+
+        def bias_matmul():
+            pb = bank("y0")
+            nc.tensor.matmul(out=pb[:], lhsT=ones[:], rhs=brow[:], start=True, stop=True)
+            T["pb"] = pb
+
+        def transposes(src, n, tag):
+            t = bank(tag)
+            for h in range(2):
+                words = src[:, 2 * n + h, :].bitcast(F32)
+                for u in range(2):
+                    col = u * 256 + h * P
+                    nc.tensor.transpose(t[:, col:col + P], words[:, u:2 * P:2], ident[:])
+            T[(tag, n)] = t
+
+        def tmod(n):
+            transposes(m_sb, n, "mt")
+
+        def tx(n):
+            transposes(x_sb, n, "xt")
+
+        def cmod(n):
+            g = work.tile([P, 1024], BF16, name="mg", tag="mg", bufs=3, align_bytes=64)
+            copy_on(
+                n not in CMOD_S,
+                g[:].bitcast(F32).rearrange("p (t u) -> p t u", u=2),
+                T[("mt", n)][:].rearrange("p (u t) -> p t u", u=2),
+            )
+            T[("mg", n)] = g
+
+        def qm(n):
+            codes = work.tile([P, 256], U32, name="m_codes", tag="m_codes", bufs=3, align_bytes=64)
+            scales = work.tile([P, 256], U8, name="m_scales", tag="m_scales", bufs=3, align_bytes=64)
+            nc.vector.quantize_mx(out=codes[:].bitcast(FP8X4), scales=scales[:], in_=T[("mg", n)][:])
+            T[("m", n)] = (codes, scales)
+
+        def s1(n):
+            codes, scales = T[("m", n)]
+            banks = (bank("sa"), bank("sb"))
+            for c in range(4):
+                nc.tensor.matmul_mx(
+                    out=banks[c // 2][:, (c % 2) * 256:(c % 2) * 256 + 256],
+                    lhsT=mw_codes[:, c * P:(c + 1) * P].bitcast(FP8X4),
+                    lhsT_scale=mw_scales[:, c * P:(c + 1) * P],
+                    rhs=codes[:].bitcast(FP8X4),
+                    rhs_scale=scales[:],
+                    start=True,
+                    stop=True,
+                )
+            T[("sp", n)] = banks
+
+        def sout(n):
+            banks = T[("sp", n)]
+            s = work.tile([P, 4, 256], F32, name="s_cm", tag="s_cm")
+            for c in range(4):
+                nc.scalar.activation(
+                    out=s[:, c, :],
+                    in_=banks[c // 2][:, (c % 2) * 256:(c % 2) * 256 + 256],
+                    func=ACT.Identity,
+                    bias=modb[:, c:c + 1],
+                    scale=1.0,
+                )
+            T[("s", n)] = s
+            T[("g", n)] = work.tile([P, 2048], BF16, name="g2", tag="g2", bufs=3, align_bytes=64)
+
+        def xs(n):
+            nc.vector.tensor_tensor(
+                out=T[("g", n)][:, 0:1024].rearrange("p (t u e) -> p t u e", u=2, e=2),
+                in0=T[("s", n)][:].rearrange("p (u e) t -> p t u e", u=2),
+                in1=T[("xt", n)][:].bitcast(BF16).rearrange("p (u t e) -> p t u e", u=2, e=2),
+                op=ALU.mult,
+            )
+
+        def ss(n):
+            sv = T[("s", n)][:].rearrange("p c (b i) -> p b c i", i=4)
+            gv = T[("g", n)][:, 1024:2048].rearrange("p (b i c) -> p b c i", i=4, c=4)
+            nc.scalar.activation(out=gv, in_=sv, func=ACT.Square)
+
+        def quant2(n):
+            codes = work.tile([P, 512], U32, name="g_codes", tag="g_codes", bufs=3, align_bytes=64)
+            scales = work.tile([P, 512], U8, name="g_scales", tag="g_scales", bufs=3, align_bytes=64)
+            nc.vector.quantize_mx(out=codes[:].bitcast(FP8X4), scales=scales[:], in_=T[("g", n)][:])
+            T[("c", n)] = (codes, scales)
+
+        def s2(n, h, which):
+            codes, scales = T[("c", n)]
+            t = bank(which + "%d" % h)
+            lo = (256 if which == "q" else 0) + h * P
+            nc.tensor.matmul_mx(
+                out=t[:],
+                lhsT=codes[:, lo:lo + P].bitcast(FP8X4),
+                lhsT_scale=scales[:, lo:lo + P],
+                rhs=(w2_codes if which == "q" else w_codes)[:].bitcast(FP8X4),
+                rhs_scale=(w2_scales if which == "q" else w_scales)[:],
+                start=True,
+                stop=True,
+            )
+            T[(which, n, h)] = t
+
+        def rs(n):
+            d = work.tile([P, 2, DIM], F32, name="d", tag="d")
+            for h in range(2):
+                nc.scalar.activation(out=d[:, h, :], in_=T[("q", n, h)][:], func=ACT.Abs_reciprocal_sqrt, bias=1e-8, scale=1.0)
+            T[("d", n)] = d
+            T[("z", n)] = work.tile([P, 2, DIM], F32, name="z", tag="z", bufs=3)
+            T[("o", n)] = work.tile([P, 2, DIM], F32, name="o", tag="o", bufs=3)
+
+        def mul(n, h):
+            nc.vector.tensor_tensor(out=T[("z", n)][:, h, :], in0=T[("y", n, h)][:], in1=T[("d", n)][:, h, :], op=ALU.mult)
+
+        def add(eng, n, h):
+            eng.tensor_tensor(out=T[("o", n)][:, h, :], in0=T[("z", n)][:, h, :], in1=bias_bc[:], op=ALU.add)
+
+        def store(n, lo, hi):
+            nc.sync.dma_start(out=ov[:, 2 * n + lo:2 * n + hi, :], in_=T[("o", n)][:, lo:hi, :])
+
+        def ok(n):
+            return 0 <= n < NU
+
+        def idle_matmuls(count, tag, rhs):
+            t = bank(tag)
+            for i in range(count):
+                nc.tensor.matmul(out=t[:], lhsT=ones[:], rhs=rhs, start=True, stop=True)
+
+        idle_matmuls(WARM_A, "sa", dz[:])
+        tmod(0)
+        mw_transposes(0)
+        mw_transposes(1)
+        cmod(0)
+        mw_copy(0, True)
+        idle_matmuls(WARM_B, "sb", mwg[:, 0:DIM])
+        mw_copy(1, False)
+        qm(0)
+        mw_quant(0)
+        mw_quant(1)
+        nc.vector.tensor_copy(out=modb[:], in_=mb_raw[:])
+        w_transposes()
+        s1(0)
+        tmod(1)
+        tx(0)
+        w_copy(0, True)
+        w_copy(1, False)
+        sout(0)
+        w_square(0)
+        cmod(1)
+        tmod(2)
+        w_square(1)
+        qm(1)
+        nc.vector.quantize_mx(out=w_codes[:].bitcast(FP8X4), scales=w_scales[:], in_=wg[:])
+        nc.vector.quantize_mx(out=w2_codes[:].bitcast(FP8X4), scales=w2_scales[:], in_=w2g[:])
+        bias_matmul()
+        s1(1)
+        xs(0)
+        ss(0)
+        tx(1)
+        nc.scalar.copy(out=bias_bc[:], in_=T["pb"][:])
+        sout(1)
+        cmod(2)
+        tmod(3)
+        qm(2)
+        if PIN_LOOP and not PIN_START:
+            ctx.enter_context(tc.manual_schedule())
+        for k in range(-1, NU):
+            if ok(k):
+                rs(k)
+            if ok(k + 1):
+                quant2(k + 1)
+            if ok(k + 3):
+                s1(k + 3)
+            if ok(k + 1):
+                s2(k + 1, 0, "q")
+                s2(k + 1, 1, "q")
+            if ok(k):
+                mul(k, 0)
+                if (k, 0) not in LATE_V:
+                    add(nc.gpsimd, k, 0)
+            if ok(k + 1):
+                s2(k + 1, 0, "y")
+            if ok(k + 4):
+                cmod(k + 4)
+            if ok(k + 5):
+                tmod(k + 5)
+            if ok(k + 2):
+                ss(k + 2)
+                xs(k + 2)
+            if ok(k + 3):
+                tx(k + 3)
+            if ok(k):
+                mul(k, 1)
+                if (k, 1) not in LATE_V:
+                    add(nc.gpsimd, k, 1)
+            if ok(k + 1):
+                s2(k + 1, 1, "y")
+            if ok(k):
+                if (k, 0) not in LATE_V and (k, 1) not in LATE_V:
+                    store(k, 0, 2)
+                elif (k, 0) not in LATE_V:
+                    store(k, 0, 1)
+            if ok(k + 3):
+                sout(k + 3)
+            if ok(k + 4):
+                qm(k + 4)
+        for n, h in LATE_V:
+            add(nc.vector, n, h)
+            store(n, h, h + 1)

@@ -148,20 +148,19 @@ def tile_modulatedlinear_kernel(tc, x, modulation, weight, bias, mod_w, mod_b, o
             nc.tensor.matmul(out=pb[:], lhsT=ones[:], rhs=brow[:], start=True, stop=True)
             T["pb"] = pb
 
-        def transposes(src, n, tag):
+        def transposes(src, n, tag, place):
             t = bank(tag)
             for h in range(2):
                 words = src[:, 2 * n + h, :].bitcast(F32)
                 for u in range(2):
-                    col = u * 256 + h * P
-                    nc.tensor.transpose(t[:, col:col + P], words[:, u:2 * P:2], ident[:])
+                    nc.tensor.transpose(t[:, place(h, u)], words[:, u:2 * P:2], ident[:])
             T[(tag, n)] = t
 
         def tmod(n):
-            transposes(m_sb, n, "mt")
+            transposes(m_sb, n, "mt", lambda h, u: slice(u * 256 + h * P, u * 256 + h * P + P))
 
         def tx(n):
-            transposes(x_sb, n, "xt")
+            transposes(x_sb, n, "xt", lambda h, u: slice(h * 256 + u, h * 256 + 256, 2))
 
         def cmod(n):
             g = work.tile([P, 1024], BF16, name="mg", tag="mg", bufs=3, align_bytes=64)
@@ -209,9 +208,9 @@ def tile_modulatedlinear_kernel(tc, x, modulation, weight, bias, mod_w, mod_b, o
 
         def xs(n):
             nc.vector.tensor_tensor(
-                out=T[("g", n)][:, 0:1024].rearrange("p (t u e) -> p t u e", u=2, e=2),
-                in0=T[("s", n)][:].rearrange("p (u e) t -> p t u e", u=2),
-                in1=T[("xt", n)][:].bitcast(BF16).rearrange("p (u t e) -> p t u e", u=2, e=2),
+                out=T[("g", n)][:, 0:1024].rearrange("p (b i c) -> p b c i", i=4, c=4),
+                in0=T[("s", n)][:].rearrange("p c (b i) -> p b c i", i=4),
+                in1=T[("xt", n)][:].bitcast(BF16).rearrange("p (b i c) -> p b c i", i=4, c=4),
                 op=ALU.mult,
             )
 

@@ -22,7 +22,7 @@ WARM_B = 2
 PIN_START = False
 PIN_LOOP = True
 LATE_V = ((6, 1), (7, 0), (7, 1))
-CMOD_S = (0,)
+CMOD_S = (0, 5, 7)
 
 
 def tile_modulatedlinear_kernel(tc, x, modulation, weight, bias, mod_w, mod_b, out):

@@ -18,11 +18,9 @@ NU = 8
 FLOPS = 3 * 2 * 2048 * 512 * 512
 
 WARM_A = 4
-WARM_B = 2
-PIN_START = False
-PIN_LOOP = True
-LATE_V = ((6, 1), (7, 0), (7, 1))
-CMOD_S = (0, 5, 7)
+LATE_V = ((7, 0), (7, 1))
+GAP_V = 6
+CMOD_S = (0, 1, 5)
 
 
 def tile_modulatedlinear_kernel(tc, x, modulation, weight, bias, mod_w, mod_b, out):
@@ -31,8 +29,6 @@ def tile_modulatedlinear_kernel(tc, x, modulation, weight, bias, mod_w, mod_b, o
         const = ctx.enter_context(tc.tile_pool(name="const", bufs=1))
         work = ctx.enter_context(tc.tile_pool(name="work", bufs=2))
         psum = ctx.enter_context(tc.psum_pool(name="psum", bufs=1))
-        if PIN_START:
-            ctx.enter_context(tc.manual_schedule())
 
         xv = x.flatten_outer_dims().rearrange("(p j) i -> p j i", j=NT)
         mv = modulation.flatten_outer_dims().rearrange("(p j) i -> p j i", j=NT)
@@ -62,11 +58,11 @@ def tile_modulatedlinear_kernel(tc, x, modulation, weight, bias, mod_w, mod_b, o
         def load_x(lo, hi):
             nc.sync.dma_start(out=x_sb[:, lo:hi, :], in_=xv[:, lo:hi, :])
 
-        load_m(0, 2)
         for u in range(2):
             nc.sync.dma_start(out=mw_sb[:, 2 * u:2 * u + 2, :], in_=mwv[:, 2 * u:2 * u + 2, :])
+        nc.sync.dma_start(out=brow[0:1, :], in_=bias.rearrange("(a n) -> a n", a=1))
+        load_m(0, 2)
         nc.scalar.dma_start(out=mb_raw[:], in_=mod_b.rearrange("(p c) -> p c", c=4))
-        nc.scalar.dma_start(out=brow[0:1, :], in_=bias.rearrange("(a n) -> a n", a=1))
         nc.scalar.activation(out=warm[:], in_=warm[:], func=ACT.Abs_reciprocal_sqrt, bias=1e-8, scale=1.0)
         nc.sync.dma_start(out=w_sb[:], in_=weight.rearrange("(c p) i -> p c i", p=P))
         load_m(2, 4)
@@ -144,7 +140,7 @@ def tile_modulatedlinear_kernel(tc, x, modulation, weight, bias, mod_w, mod_b, o
             nc.vector.tensor_tensor(out=w2g[:, half], in0=wg[:, half], in1=wg[:, half], op=ALU.mult)
 
         def bias_matmul():
-            pb = bank("y0")
+            pb = bank("sb")
             nc.tensor.matmul(out=pb[:], lhsT=ones[:], rhs=brow[:], start=True, stop=True)
             T["pb"] = pb
 
@@ -266,43 +262,41 @@ def tile_modulatedlinear_kernel(tc, x, modulation, weight, bias, mod_w, mod_b, o
                 nc.tensor.matmul(out=t[:], lhsT=ones[:], rhs=rhs, start=True, stop=True)
 
         idle_matmuls(WARM_A, "sa", dz[:])
-        tmod(0)
+        ctx.enter_context(tc.manual_schedule())
         mw_transposes(0)
         mw_transposes(1)
-        cmod(0)
+        tmod(0)
+        bias_matmul()
         mw_copy(0, True)
-        idle_matmuls(WARM_B, "sb", mwg[:, 0:DIM])
         mw_copy(1, False)
-        qm(0)
         mw_quant(0)
+        cmod(0)
         mw_quant(1)
+        qm(0)
+        nc.scalar.copy(out=bias_bc[:], in_=T["pb"][:])
         nc.vector.tensor_copy(out=modb[:], in_=mb_raw[:])
         w_transposes()
-        s1(0)
         tmod(1)
-        tx(0)
         w_copy(0, True)
         w_copy(1, False)
-        sout(0)
-        w_square(0)
         cmod(1)
+        s1(0)
+        sout(0)
+        tx(0)
         tmod(2)
+        w_square(0)
         w_square(1)
         qm(1)
-        nc.vector.quantize_mx(out=w_codes[:].bitcast(FP8X4), scales=w_scales[:], in_=wg[:])
-        nc.vector.quantize_mx(out=w2_codes[:].bitcast(FP8X4), scales=w2_scales[:], in_=w2g[:])
-        bias_matmul()
         s1(1)
+        nc.vector.quantize_mx(out=w_codes[:].bitcast(FP8X4), scales=w_scales[:], in_=wg[:])
         xs(0)
         ss(0)
-        tx(1)
-        nc.scalar.copy(out=bias_bc[:], in_=T["pb"][:])
-        sout(1)
         cmod(2)
+        tx(1)
         tmod(3)
+        nc.vector.quantize_mx(out=w2_codes[:].bitcast(FP8X4), scales=w2_scales[:], in_=w2g[:])
+        sout(1)
         qm(2)
-        if PIN_LOOP and not PIN_START:
-            ctx.enter_context(tc.manual_schedule())
         for k in range(-1, NU):
             if ok(k):
                 rs(k)
@@ -315,7 +309,7 @@ def tile_modulatedlinear_kernel(tc, x, modulation, weight, bias, mod_w, mod_b, o
                 s2(k + 1, 1, "q")
             if ok(k):
                 mul(k, 0)
-                if (k, 0) not in LATE_V:
+                if (k, 0) not in LATE_V and k != GAP_V:
                     add(nc.gpsimd, k, 0)
             if ok(k + 1):
                 s2(k + 1, 0, "y")
@@ -332,13 +326,16 @@ def tile_modulatedlinear_kernel(tc, x, modulation, weight, bias, mod_w, mod_b, o
                 mul(k, 1)
                 if (k, 1) not in LATE_V:
                     add(nc.gpsimd, k, 1)
+                if k == GAP_V:
+                    add(nc.vector, k, 0)
             if ok(k + 1):
                 s2(k + 1, 1, "y")
             if ok(k):
-                if (k, 0) not in LATE_V and (k, 1) not in LATE_V:
+                if k < GAP_V:
                     store(k, 0, 2)
-                elif (k, 0) not in LATE_V:
+                elif k == GAP_V:
                     store(k, 0, 1)
+                    store(k, 1, 2)
             if ok(k + 3):
                 sout(k + 3)
             if ok(k + 4):

@@ -64,7 +64,9 @@ def tile_modulatedlinear_kernel(tc, x, modulation, weight, bias, mod_w, mod_b, o
         load_m(0, 2)
         nc.scalar.dma_start(out=mb_raw[:], in_=mod_b.rearrange("(p c) -> p c", c=4))
         nc.scalar.activation(out=warm[:], in_=warm[:], func=ACT.Abs_reciprocal_sqrt, bias=1e-8, scale=1.0)
-        nc.sync.dma_start(out=w_sb[:], in_=weight.rearrange("(c p) i -> p c i", p=P))
+        wv = weight.rearrange("(c p) i -> p c i", p=P)
+        for b in range(2):
+            nc.sync.dma_start(out=w_sb[:, 2 * b:2 * b + 2, :], in_=wv[:, 2 * b:2 * b + 2, :])
         load_m(2, 4)
         load_x(0, 2)
         load_x(2, 4)
@@ -76,7 +78,6 @@ def tile_modulatedlinear_kernel(tc, x, modulation, weight, bias, mod_w, mod_b, o
         def bank(tag):
             return psum.tile([P, 512], F32, name=tag, tag=tag)
 
-        modb = const.tile([P, 4], F32, name="modb")
         mwg = const.tile([P, 2048], BF16, name="mwg", align_bytes=64)
         mw_codes = const.tile([P, 512], U32, name="mw_codes", align_bytes=64)
         mw_scales = const.tile([P, 512], U8, name="mw_scales", align_bytes=64)
@@ -196,7 +197,7 @@ def tile_modulatedlinear_kernel(tc, x, modulation, weight, bias, mod_w, mod_b, o
                     out=s[:, c, :],
                     in_=banks[c // 2][:, (c % 2) * 256:(c % 2) * 256 + 256],
                     func=ACT.Identity,
-                    bias=modb[:, c:c + 1],
+                    bias=mb_raw[:, c:c + 1],
                     scale=1.0,
                 )
             T[("s", n)] = s
@@ -274,7 +275,6 @@ def tile_modulatedlinear_kernel(tc, x, modulation, weight, bias, mod_w, mod_b, o
         mw_quant(1)
         qm(0)
         nc.scalar.copy(out=bias_bc[:], in_=T["pb"][:])
-        nc.vector.tensor_copy(out=modb[:], in_=mb_raw[:])
         w_transposes()
         tmod(1)
         w_copy(0, True)

@@ -18,6 +18,7 @@ NU = 8
 FLOPS = 3 * 2 * 2048 * 512 * 512
 
 WARM_A = 4
+WARM_B = 2
 LATE_V = ((7, 0), (7, 1))
 GAP_V = 6
 CMOD_S = (0, 1, 5)
@@ -268,6 +269,7 @@ def tile_modulatedlinear_kernel(tc, x, modulation, weight, bias, mod_w, mod_b, o
         mw_transposes(1)
         tmod(0)
         bias_matmul()
+        idle_matmuls(WARM_B, "sa", dz[:])
         mw_copy(0, True)
         mw_copy(1, False)
         mw_quant(0)

from contextlib import ExitStack

import concourse.mybir as mybir
from concourse.masks import make_identity

F32 = mybir.dt.float32
BF16 = mybir.dt.bfloat16
U32 = mybir.dt.uint32
U8 = mybir.dt.uint8
FP8X4 = mybir.dt.float8_e4m3fn_x4
ACT = mybir.ActivationFunctionType
ALU = mybir.AluOpType

P = 128
DIM = 512
NT = 16
NU = 8
FLOPS = 3 * 2 * 2048 * 512 * 512

WARM_A = 4
WARM_B = 2
LATE_V = ((7, 0), (7, 1))
GAP_V = 6
CMOD_S = (0, 1, 5)


def tile_modulatedlinear_kernel(tc, x, modulation, weight, bias, mod_w, mod_b, out):
    nc = tc.nc
    with ExitStack() as ctx:
        const = ctx.enter_context(tc.tile_pool(name="const", bufs=1))
        work = ctx.enter_context(tc.tile_pool(name="work", bufs=2))
        psum = ctx.enter_context(tc.psum_pool(name="psum", bufs=1))

        xv = x.flatten_outer_dims().rearrange("(p j) i -> p j i", j=NT)
        mv = modulation.flatten_outer_dims().rearrange("(p j) i -> p j i", j=NT)
        ov = out.flatten_outer_dims().rearrange("(p j) o -> p j o", j=NT)
        mwv = mod_w.rearrange("(p c) m -> p c m", c=4)

        x_sb = const.tile([P, NT, DIM], BF16, name="x_sb")
        m_sb = const.tile([P, NT, DIM], BF16, name="m_sb")
        mw_sb = const.tile([P, 4, DIM], BF16, name="mw_sb")
        w_sb = const.tile([P, 4, DIM], BF16, name="w_sb")
        mb_raw = const.tile([P, 4], BF16, name="mb_raw")
        brow = const.tile([P, DIM], BF16, name="brow")
        ones = const.tile([P, P], BF16, name="ones")
        ident = const.tile([P, P], F32, name="ident")
        warm = const.tile([P, 1], F32, name="warm")
        dz = const.tile([P, DIM], BF16, name="dz")

        nc.vector.memset(ones[:], 1.0)
        nc.vector.memset(dz[:], 0.0)
        nc.vector.memset(warm[:], 1.0)
        make_identity(nc, ident[:])
        nc.vector.memset(brow[:], 0.0)

        def load_m(lo, hi):
            nc.sync.dma_start(out=m_sb[:, lo:hi, :], in_=mv[:, lo:hi, :])

        def load_x(lo, hi):
            nc.sync.dma_start(out=x_sb[:, lo:hi, :], in_=xv[:, lo:hi, :])

        for u in range(2):
            nc.sync.dma_start(out=mw_sb[:, 2 * u:2 * u + 2, :], in_=mwv[:, 2 * u:2 * u + 2, :])
        nc.sync.dma_start(out=brow[0:1, :], in_=bias.rearrange("(a n) -> a n", a=1))
        load_m(0, 2)
        nc.scalar.dma_start(out=mb_raw[:], in_=mod_b.rearrange("(p c) -> p c", c=4))
        nc.scalar.activation(out=warm[:], in_=warm[:], func=ACT.Abs_reciprocal_sqrt, bias=1e-8, scale=1.0)
        wv = weight.rearrange("(c p) i -> p c i", p=P)
        for b in range(2):
            nc.sync.dma_start(out=w_sb[:, 2 * b:2 * b + 2, :], in_=wv[:, 2 * b:2 * b + 2, :])
        load_m(2, 4)
        load_x(0, 2)
        load_x(2, 4)
        load_m(4, 8)
        load_x(4, 8)
        load_m(8, 16)
        load_x(8, 16)

        def bank(tag):
            return psum.tile([P, 512], F32, name=tag, tag=tag)

        mwg = const.tile([P, 2048], BF16, name="mwg", align_bytes=64)
        mw_codes = const.tile([P, 512], U32, name="mw_codes", align_bytes=64)
        mw_scales = const.tile([P, 512], U8, name="mw_scales", align_bytes=64)
        wg = const.tile([P, 2048], BF16, name="wg", align_bytes=64)
        w2g = const.tile([P, 2048], BF16, name="w2g", align_bytes=64)
        w_codes = const.tile([P, 512], U32, name="w_codes", align_bytes=64)
        w_scales = const.tile([P, 512], U8, name="w_scales", align_bytes=64)
        w2_codes = const.tile([P, 512], U32, name="w2_codes", align_bytes=64)
        w2_scales = const.tile([P, 512], U8, name="w2_scales", align_bytes=64)
        bias_bc = const.tile([P, DIM], F32, name="bias_bc")

        T = {}

        def copy_on(vector, dst, src):
            if vector:
                nc.vector.tensor_copy(out=dst, in_=src)
            else:
                nc.scalar.copy(out=dst, in_=src)

        def mw_transposes(b):
            t = bank(("y0", "q0")[b])
            for c2 in range(2):
                words = mw_sb[:, 2 * b + c2, :].bitcast(F32)
                for v in range(2):
                    col = (c2 * 2 + v) * P
                    nc.tensor.transpose(t[:, col:col + P], words[:, v:2 * P:2], ident[:])
            T[("mwt", b)] = t

        def mw_copy(b, vector):
            copy_on(
                vector,
                mwg[:].bitcast(F32)[:, b * 512:(b + 1) * 512].rearrange("p (c i v) -> p c i v", c=2, v=2),
                T[("mwt", b)][:].rearrange("p (c v i) -> p c i v", c=2, v=2),
            )

        def mw_quant(b):
            nc.vector.quantize_mx(
                out=mw_codes[:, b * 256:(b + 1) * 256].bitcast(FP8X4),
                scales=mw_scales[:, b * 256:(b + 1) * 256],
                in_=mwg[:, b * 1024:(b + 1) * 1024],
            )

        def w_transposes():
            wt = [bank("y1"), bank("q1")]
            for oc in range(4):
                words = w_sb[:, oc, :].bitcast(F32)
                for u in range(2):
                    col = u * 256 + (oc % 2) * P
                    nc.tensor.transpose(wt[oc // 2][:, col:col + P], words[:, u:2 * P:2], ident[:])
            T["wt"] = wt

        def w_copy(b, vector):
            copy_on(
                vector,
                wg[:].bitcast(F32)[:, b * 512:(b + 1) * 512].rearrange("p (o u) -> p o u", u=2),
                T["wt"][b][:].rearrange("p (u o) -> p o u", u=2),
            )

        def w_square(b):
            half = slice(b * 1024, (b + 1) * 1024)
            nc.vector.tensor_tensor(out=w2g[:, half], in0=wg[:, half], in1=wg[:, half], op=ALU.mult)

        def bias_matmul():
            pb = bank("sb")
            nc.tensor.matmul(out=pb[:], lhsT=ones[:], rhs=brow[:], start=True, stop=True)
            T["pb"] = pb

        def transposes(src, n, tag, place):
            t = bank(tag)
            for h in range(2):
                words = src[:, 2 * n + h, :].bitcast(F32)
                for u in range(2):
                    nc.tensor.transpose(t[:, place(h, u)], words[:, u:2 * P:2], ident[:])
            T[(tag, n)] = t

        def tmod(n):
            transposes(m_sb, n, "mt", lambda h, u: slice(u * 256 + h * P, u * 256 + h * P + P))

        def tx(n):
            transposes(x_sb, n, "xt", lambda h, u: slice(h * 256 + u, h * 256 + 256, 2))

        def cmod(n):
            g = work.tile([P, 1024], BF16, name="mg", tag="mg", bufs=3, align_bytes=64)
            copy_on(
                n not in CMOD_S,
                g[:].bitcast(F32).rearrange("p (t u) -> p t u", u=2),
                T[("mt", n)][:].rearrange("p (u t) -> p t u", u=2),
            )
            T[("mg", n)] = g

        def qm(n):
            codes = work.tile([P, 256], U32, name="m_codes", tag="m_codes", bufs=3, align_bytes=64)
            scales = work.tile([P, 256], U8, name="m_scales", tag="m_scales", bufs=3, align_bytes=64)
            nc.vector.quantize_mx(out=codes[:].bitcast(FP8X4), scales=scales[:], in_=T[("mg", n)][:])
            T[("m", n)] = (codes, scales)

        def s1(n):
            codes, scales = T[("m", n)]
            banks = (bank("sa"), bank("sb"))
            for c in range(4):
                nc.tensor.matmul_mx(
                    out=banks[c // 2][:, (c % 2) * 256:(c % 2) * 256 + 256],
                    lhsT=mw_codes[:, c * P:(c + 1) * P].bitcast(FP8X4),
                    lhsT_scale=mw_scales[:, c * P:(c + 1) * P],
                    rhs=codes[:].bitcast(FP8X4),
                    rhs_scale=scales[:],
                    start=True,
                    stop=True,
                )
            T[("sp", n)] = banks

        def sout(n):
            banks = T[("sp", n)]
            s = work.tile([P, 4, 256], F32, name="s_cm", tag="s_cm")
            for c in range(4):
                nc.scalar.activation(
                    out=s[:, c, :],
                    in_=banks[c // 2][:, (c % 2) * 256:(c % 2) * 256 + 256],
                    func=ACT.Identity,
                    bias=mb_raw[:, c:c + 1],
                    scale=1.0,
                )
            T[("s", n)] = s
            T[("g", n)] = work.tile([P, 2048], BF16, name="g2", tag="g2", bufs=3, align_bytes=64)

        def xs(n):
            nc.vector.tensor_tensor(
                out=T[("g", n)][:, 0:1024].rearrange("p (b i c) -> p b c i", i=4, c=4),
                in0=T[("s", n)][:].rearrange("p c (b i) -> p b c i", i=4),
                in1=T[("xt", n)][:].bitcast(BF16).rearrange("p (b i c) -> p b c i", i=4, c=4),
                op=ALU.mult,
            )

        def ss(n):
            sv = T[("s", n)][:].rearrange("p c (b i) -> p b c i", i=4)
            gv = T[("g", n)][:, 1024:2048].rearrange("p (b i c) -> p b c i", i=4, c=4)
            nc.scalar.activation(out=gv, in_=sv, func=ACT.Square)

        def quant2(n):
            codes = work.tile([P, 512], U32, name="g_codes", tag="g_codes", bufs=3, align_bytes=64)
            scales = work.tile([P, 512], U8, name="g_scales", tag="g_scales", bufs=3, align_bytes=64)
            nc.vector.quantize_mx(out=codes[:].bitcast(FP8X4), scales=scales[:], in_=T[("g", n)][:])
            T[("c", n)] = (codes, scales)

        def s2(n, h, which):
            codes, scales = T[("c", n)]
            t = bank(which + "%d" % h)
            lo = (256 if which == "q" else 0) + h * P
            nc.tensor.matmul_mx(
                out=t[:],
                lhsT=codes[:, lo:lo + P].bitcast(FP8X4),
                lhsT_scale=scales[:, lo:lo + P],
                rhs=(w2_codes if which == "q" else w_codes)[:].bitcast(FP8X4),
                rhs_scale=(w2_scales if which == "q" else w_scales)[:],
                start=True,
                stop=True,
            )
            T[(which, n, h)] = t

        def rs(n):
            d = work.tile([P, 2, DIM], F32, name="d", tag="d")
            for h in range(2):
                nc.scalar.activation(out=d[:, h, :], in_=T[("q", n, h)][:], func=ACT.Abs_reciprocal_sqrt, bias=1e-8, scale=1.0)
            T[("d", n)] = d
            T[("z", n)] = work.tile([P, 2, DIM], F32, name="z", tag="z", bufs=3)
            T[("o", n)] = work.tile([P, 2, DIM], F32, name="o", tag="o", bufs=3)

        def mul(n, h):
            nc.vector.tensor_tensor(out=T[("z", n)][:, h, :], in0=T[("y", n, h)][:], in1=T[("d", n)][:, h, :], op=ALU.mult)

        def add(eng, n, h):
            eng.tensor_tensor(out=T[("o", n)][:, h, :], in0=T[("z", n)][:, h, :], in1=bias_bc[:], op=ALU.add)

        def store(n, lo, hi):
            nc.sync.dma_start(out=ov[:, 2 * n + lo:2 * n + hi, :], in_=T[("o", n)][:, lo:hi, :])

        def ok(n):
            return 0 <= n < NU

        def idle_matmuls(count, tag, rhs):
            t = bank(tag)
            for i in range(count):
                nc.tensor.matmul(out=t[:], lhsT=ones[:], rhs=rhs, start=True, stop=True)

        idle_matmuls(WARM_A, "sa", dz[:])
        ctx.enter_context(tc.manual_schedule())
        mw_transposes(0)
        mw_transposes(1)
        tmod(0)
        bias_matmul()
        idle_matmuls(WARM_B, "sa", dz[:])
        mw_copy(0, True)
        mw_copy(1, False)
        mw_quant(0)
        cmod(0)
        mw_quant(1)
        qm(0)
        nc.scalar.copy(out=bias_bc[:], in_=T["pb"][:])
        w_transposes()
        tmod(1)
        w_copy(0, True)
        w_copy(1, False)
        cmod(1)
        s1(0)
        sout(0)
        tx(0)
        tmod(2)
        w_square(0)
        w_square(1)
        qm(1)
        s1(1)
        nc.vector.quantize_mx(out=w_codes[:].bitcast(FP8X4), scales=w_scales[:], in_=wg[:])
        xs(0)
        ss(0)
        cmod(2)
        tx(1)
        tmod(3)
        nc.vector.quantize_mx(out=w2_codes[:].bitcast(FP8X4), scales=w2_scales[:], in_=w2g[:])
        sout(1)
        qm(2)
        for k in range(-1, NU):
            if ok(k):
                rs(k)
            if ok(k + 1):
                quant2(k + 1)
            if ok(k + 3):
                s1(k + 3)
            if ok(k + 1):
                s2(k + 1, 0, "q")
                s2(k + 1, 1, "q")
            if ok(k):
                mul(k, 0)
                if (k, 0) not in LATE_V and k != GAP_V:
                    add(nc.gpsimd, k, 0)
            if ok(k + 1):
                s2(k + 1, 0, "y")
            if ok(k + 4):
                cmod(k + 4)
            if ok(k + 5):
                tmod(k + 5)
            if ok(k + 2):
                ss(k + 2)
                xs(k + 2)
            if ok(k + 3):
                tx(k + 3)
            if ok(k):
                mul(k, 1)
                if (k, 1) not in LATE_V:
                    add(nc.gpsimd, k, 1)
                if k == GAP_V:
                    add(nc.vector, k, 0)
            if ok(k + 1):
                s2(k + 1, 1, "y")
            if ok(k):
                if k < GAP_V:
                    store(k, 0, 2)
                elif k == GAP_V:
                    store(k, 0, 1)
                    store(k, 1, 2)
            if ok(k + 3):
                sout(k + 3)
            if ok(k + 4):
                qm(k + 4)
        for n, h in LATE_V:
            add(nc.vector, n, h)
            store(n, h, h + 1)
